import numpy as np
import ml_dtypes


def mxq(x, axis, fmt="e4m3"):
    dtype, down = {"e4m3": (ml_dtypes.float8_e4m3fn, 7), "e5m2": (ml_dtypes.float8_e5m2, 14)}[fmt]
    v = np.moveaxis(np.asarray(x, np.float32).astype(ml_dtypes.bfloat16).astype(np.float64), axis, -1)
    blocks = v.reshape(v.shape[:-1] + (-1, 32))
    amax = np.abs(blocks).max(-1, keepdims=True)
    byte = np.maximum(np.where(amax > 0, np.frexp(amax)[1] - 1 + 127, 0) - down, 1)
    scale = np.exp2(byte - 127.0)
    codes = (blocks / scale).astype(np.float32).astype(dtype).astype(np.float64)
    return np.moveaxis((codes * scale).reshape(v.shape), -1, axis)


WIDE = False


def mx_kscale(k):
    if not WIDE:
        return np.ones(k)
    levels = np.array([10, -10, 5, -5, 0])
    a = np.random.permutation(np.resize(levels, k // 512 * 4)).reshape(k // 512, 4)
    idx = np.arange(k)
    return np.exp2(a[idx // 512, idx % 128 // 32])


BF16 = ml_dtypes.bfloat16


def bf(x):
    return np.asarray(x, np.float32).astype(BF16)


def f64(x):
    return np.asarray(x).astype(np.float64)


E, F, H, MID, OUT = 16384, 64, 192, 512, 128
D = 2 * (F + H)
IN = D + 1


def setup_inputs():
    s = mx_kscale(D)
    t = mx_kscale(MID)
    w1 = np.concatenate([np.random.standard_normal((MID, D)) / np.sqrt(D) / s[None, :],
                         np.random.standard_normal((MID, 1)) * 0.5], axis=1) * t[:, None]
    return {"dst_node_feat": bf(np.random.standard_normal((E, F)) * s[:F]),
            "dst_node_hidden": bf(np.random.standard_normal((E, H)) * s[F:F + H]),
            "src_node_feat": bf(np.random.standard_normal((E, F)) * s[F + H:2 * F + H]),
            "src_node_hidden": bf(np.random.standard_normal((E, H)) * s[2 * F + H:]),
            "edge_feat": bf(np.random.standard_normal(E)),
            "W1": bf(w1),
            "b1": bf(np.random.standard_normal(MID) * 0.3 * t),
            "W2": bf(np.random.standard_normal((OUT, MID)) / np.sqrt(MID) / t[None, :]),
            "b2": bf(np.random.standard_normal(OUT) * 0.3)}


def reference(dst_node_feat, dst_node_hidden, src_node_feat, src_node_hidden, edge_feat, W1, b1, W2, b2):
    x = np.concatenate([f64(dst_node_feat), f64(dst_node_hidden), f64(src_node_feat), f64(src_node_hidden),
                        f64(edge_feat)[:, None]], axis=1)
    w1 = f64(W1)
    pre = (mxq(x[:, :D], 1, "e4m3") @ mxq(w1[:, :D], 1, "e4m3").T) + x[:, D:] * w1[:, D] + f64(b1)
    h = np.maximum(pre, 0.0)
    return np.tanh((mxq(h, 1, "e4m3") @ mxq(f64(W2), 1, "e4m3").T) + f64(b2))

@@ -1,0 +1,279 @@
+from contextlib import ExitStack
+
+import concourse.mybir as mybir
+from concourse.masks import make_identity
+
+F32 = mybir.dt.float32
+BF16 = mybir.dt.bfloat16
+U32 = mybir.dt.uint32
+U8 = mybir.dt.uint8
+FP8X4 = mybir.dt.float8_e4m3fn_x4
+ACT = mybir.ActivationFunctionType
+ALU = mybir.AluOpType
+
+P = 128
+PACK = 4
+E, F, H, MID, OUT = 16384, 64, 192, 512, 128
+D = 2 * (F + H)
+M_TILES = MID // P
+CHUNK = 512
+SUBS = CHUNK // P
+N_CHUNKS = E // CHUNK
+BLOCK = 1024
+CHUNKS_PER_BLOCK = BLOCK // CHUNK
+N_BLOCKS = E // BLOCK
+BLOCKS_AHEAD = 2
+EDGE_PIECES = 4
+SCALAR_M_TILES = 2
+
+FLOPS = 2 * E * ((D + 1) * MID + MID * OUT)
+
+
+def tile_edgenetwork_kernel(
+    tc,
+    dst_node_feat,
+    dst_node_hidden,
+    src_node_feat,
+    src_node_hidden,
+    edge_feat,
+    W1,
+    b1,
+    W2,
+    b2,
+    out,
+):
+    nc = tc.nc
+    with ExitStack() as stack:
+        stack.enter_context(tc.manual_schedule())
+        const = stack.enter_context(tc.tile_pool(name="const", bufs=1))
+        rows_pool = stack.enter_context(tc.tile_pool(name="rows", bufs=BLOCKS_AHEAD + 1))
+        term_pool = stack.enter_context(tc.tile_pool(name="term", bufs=3))
+        work = stack.enter_context(tc.tile_pool(name="work", bufs=2))
+        store_pool = stack.enter_context(tc.tile_pool(name="store", bufs=3))
+        flip_psum = stack.enter_context(tc.psum_pool(name="flip_psum", bufs=2))
+        layer1_psum = stack.enter_context(tc.psum_pool(name="layer1_psum", bufs=SUBS))
+        layer2_psum = stack.enter_context(tc.psum_pool(name="layer2_psum", bufs=1))
+        back_psum = stack.enter_context(tc.psum_pool(name="back_psum", bufs=1))
+
+        x_parts = (
+            (dst_node_feat, 0, F),
+            (dst_node_hidden, F, H),
+            (src_node_feat, F + H, F),
+            (src_node_hidden, 2 * F + H, H),
+        )
+        x_blocks = {}
+
+        def load_block(b):
+            x_rows = rows_pool.tile([P, BLOCK // P, D], BF16)
+            for part, first, width in x_parts:
+                nc.sync.dma_start(
+                    out=x_rows[:, :, first : first + width],
+                    in_=part[b * BLOCK : (b + 1) * BLOCK, :].rearrange("(r p) c -> p r c", p=P),
+                )
+            x_blocks[b] = x_rows
+
+        w1_rows = const.tile([P, M_TILES, D + 2], BF16)
+        nc.sync.dma_start(out=w1_rows[:, :, 0 : D + 1], in_=W1.rearrange("(t p) k -> p t k", p=P))
+        load_block(0)
+        w2_rows = const.tile([P, MID], BF16)
+        nc.sync.dma_start(out=w2_rows[:], in_=W2)
+        bias_rows = const.tile([P, P], BF16)
+        nc.vector.memset(bias_rows[:], 0.0)
+        nc.sync.dma_start(out=bias_rows[0:M_TILES, :], in_=b1.rearrange("(t p) -> t p", p=P))
+        nc.sync.dma_start(out=bias_rows[M_TILES : M_TILES + 1, :], in_=b2.rearrange("(o p) -> o p", p=P))
+        for b in range(1, BLOCKS_AHEAD):
+            load_block(b)
+
+        edge_all = const.tile([P, E], BF16)
+        piece = E // EDGE_PIECES
+        for q in range(EDGE_PIECES):
+            nc.scalar.dma_start(
+                out=edge_all[:, q * piece : (q + 1) * piece],
+                in_=edge_feat[q * piece : (q + 1) * piece].partition_broadcast(P),
+            )
+
+        ident_f32 = const.tile([P, P], F32)
+        make_identity(nc, ident_f32[:])
+        ident_bf16 = const.tile([P, P], BF16)
+        make_identity(nc, ident_bf16[:])
+
+        def contraction_onto_partitions(row_words, grouped):
+            grouped_words = grouped[:].bitcast(F32)
+            for half in range(SUBS // 2):
+                flipped = flip_psum.tile([P, 2, 2, P], F32)
+                for s in range(2):
+                    for u in range(2):
+                        nc.tensor.transpose(
+                            flipped[:, s, u, :], row_words(2 * half + s)[:, u * P : (u + 1) * P], ident_f32[:]
+                        )
+                nc.scalar.copy(
+                    out=grouped_words[:, 2 * half * P : (2 * half + 2) * P, :].rearrange(
+                        "p (s r) u -> p s r u", s=2
+                    ),
+                    in_=flipped[:].rearrange("p s u r -> p s r u"),
+                )
+
+        def quantise(grouped, codes, scales):
+            nc.vector.quantize_mx(
+                out=codes[:].bitcast(FP8X4), scales=scales[:], in_=grouped[:].rearrange("p c j -> p (c j)")
+            )
+
+        w1_words = w1_rows[:].bitcast(F32)
+        w1_grouped = const.tile([P, MID, PACK], BF16, align_bytes=64)
+        contraction_onto_partitions(lambda t: w1_words[:, t, 0 : D // 2], w1_grouped)
+        w1_codes = const.tile([P, MID], U32, align_bytes=64)
+        w1_scales = const.tile([P, MID], U8, align_bytes=64)
+        quantise(w1_grouped, w1_codes, w1_scales)
+
+        w2_flipped = back_psum.tile([P, M_TILES, OUT], BF16, tag="back")
+        for t in range(M_TILES):
+            nc.tensor.transpose(w2_flipped[:, t, :], w2_rows[:, t * P : (t + 1) * P], ident_bf16[:])
+        w2_grouped = const.tile([P, OUT, PACK], BF16, align_bytes=64)
+        nc.vector.tensor_copy(out=w2_grouped[:], in_=w2_flipped[:].rearrange("p t o -> p o t"))
+        w2_codes = const.tile([P, OUT], U32, align_bytes=64)
+        w2_scales = const.tile([P, OUT], U8, align_bytes=64)
+
+        bias_flipped = layer2_psum.tile([P, P], BF16, tag="layer2")
+        nc.tensor.transpose(bias_flipped[:], bias_rows[:], ident_bf16[:])
+        bias_cols = const.tile([P, M_TILES + 1], F32)
+        nc.vector.tensor_copy(out=bias_cols[:], in_=bias_flipped[:, 0 : M_TILES + 1])
+        w1_last = const.tile([P, M_TILES], F32)
+        nc.vector.tensor_copy(out=w1_last[:], in_=w1_rows[:, :, D])
+        quantise(w2_grouped, w2_codes, w2_scales)
+
+        x_grouped, x_codes, x_scales = {}, {}, {}
+        edge_terms, layer1_banks, pre_acts, hidden = {}, {}, {}, {}
+        h_codes, h_scales, out_flipped = {}, {}, {}
+
+        def flip_x(c):
+            x_words = x_blocks[c // CHUNKS_PER_BLOCK][:].bitcast(F32)
+            first = (c % CHUNKS_PER_BLOCK) * SUBS
+            grouped = work.tile([P, CHUNK, PACK], BF16, align_bytes=64, name="x_grouped")
+            contraction_onto_partitions(lambda s: x_words[:, first + s, :], grouped)
+            x_grouped[c] = grouped
+
+        def make_edge_term(c):
+            term = term_pool.tile([P, M_TILES, CHUNK], F32, name="edge_term")
+            edges = edge_all[:, c * CHUNK : (c + 1) * CHUNK]
+            for t in range(M_TILES):
+                if t < SCALAR_M_TILES:
+                    nc.scalar.activation(
+                        out=term[:, t, :],
+                        in_=edges,
+                        func=ACT.Identity,
+                        scale=w1_last[:, t : t + 1],
+                        bias=bias_cols[:, t : t + 1],
+                    )
+                else:
+                    nc.gpsimd.tensor_scalar(
+                        out=term[:, t, :],
+                        in0=edges,
+                        scalar1=w1_last[:, t : t + 1],
+                        scalar2=bias_cols[:, t : t + 1],
+                        op0=ALU.mult,
+                        op1=ALU.add,
+                    )
+            edge_terms[c] = term
+
+        def quantise_x(c):
+            codes = work.tile([P, CHUNK], U32, align_bytes=64, name="x_codes")
+            scales = work.tile([P, CHUNK], U8, align_bytes=64, name="x_scales")
+            quantise(x_grouped[c], codes, scales)
+            x_codes[c], x_scales[c] = codes, scales
+
+        def layer1(c):
+            for s in range(SUBS):
+                bank = layer1_psum.tile([P, M_TILES, P], F32, name="layer1_bank")
+                for t in range(M_TILES):
+                    nc.tensor.matmul_mx(
+                        out=bank[:, t, :],
+                        lhsT=w1_codes[:, t * P : (t + 1) * P].bitcast(FP8X4),
+                        lhsT_scale=w1_scales[:, t * P : (t + 1) * P],
+                        rhs=x_codes[c][:, s * P : (s + 1) * P].bitcast(FP8X4),
+                        rhs_scale=x_scales[c][:, s * P : (s + 1) * P],
+                        start=True,
+                        stop=True,
+                    )
+                layer1_banks[c, s] = bank
+
+        def add_edge_term(c, s):
+            if s == 0:
+                pre_acts[c] = work.tile([P, CHUNK, PACK], BF16, align_bytes=64, name="pre_act")
+            nc.vector.tensor_tensor(
+                out=pre_acts[c][:, s * P : (s + 1) * P, :],
+                in0=layer1_banks[c, s][:].rearrange("p t e -> p e t"),
+                in1=edge_terms[c][:, :, s * P : (s + 1) * P].rearrange("p t e -> p e t"),
+                op=ALU.add,
+            )
+
+        def relu(c):
+            h = work.tile([P, CHUNK, PACK], BF16, align_bytes=64, name="hidden")
+            nc.vector.tensor_scalar_max(
+                out=h[:].rearrange("p e t -> p (e t)"),
+                in0=pre_acts[c][:].rearrange("p e t -> p (e t)"),
+                scalar1=0.0,
+            )
+            hidden[c] = h
+
+        def quantise_h(c):
+            codes = work.tile([P, CHUNK], U32, align_bytes=64, name="h_codes")
+            scales = work.tile([P, CHUNK], U8, align_bytes=64, name="h_scales")
+            quantise(hidden[c], codes, scales)
+            h_codes[c], h_scales[c] = codes, scales
+
+        def layer2(c):
+            acc = layer2_psum.tile([P, CHUNK], F32, tag="layer2")
+            nc.tensor.matmul_mx(
+                out=acc[:],
+                lhsT=w2_codes[:].bitcast(FP8X4),
+                lhsT_scale=w2_scales[:],
+                rhs=h_codes[c][:].bitcast(FP8X4),
+                rhs_scale=h_scales[c][:],
+                start=True,
+                stop=True,
+            )
+            flipped = work.tile([P, CHUNK], F32, name="out_flipped")
+            nc.scalar.activation(
+                out=flipped[:], in_=acc[:], func=ACT.Tanh, bias=bias_cols[:, M_TILES : M_TILES + 1], scale=1.0
+            )
+            out_flipped[c] = flipped
+
+        def store(c):
+            back = back_psum.tile([P, SUBS, OUT], F32, tag="back")
+            for s in range(SUBS):
+                nc.tensor.transpose(back[:, s, :], out_flipped[c][:, s * P : (s + 1) * P], ident_f32[:])
+            result = store_pool.tile([P, SUBS, OUT], F32)
+            nc.scalar.copy(out=result[:], in_=back[:])
+            nc.scalar.dma_start(
+                out=out[c * CHUNK : (c + 1) * CHUNK, :].rearrange("(s p) o -> p s o", p=P), in_=result[:]
+            )
+
+        def live(c):
+            return 0 <= c < N_CHUNKS
+
+        for i in range(-2, N_CHUNKS + 2):
+            ahead = i + 2
+            if live(ahead) and ahead % CHUNKS_PER_BLOCK == 0:
+                b = ahead // CHUNKS_PER_BLOCK + BLOCKS_AHEAD
+                if b < N_BLOCKS:
+                    load_block(b)
+            if live(i - 2):
+                store(i - 2)
+            if live(i + 2):
+                flip_x(i + 2)
+            if live(i):
+                add_edge_term(i, 0)
+                add_edge_term(i, 1)
+            if live(i - 1):
+                quantise_h(i - 1)
+                layer2(i - 1)
+            if live(i):
+                add_edge_term(i, 2)
+                add_edge_term(i, 3)
+            if live(i + 1):
+                quantise_x(i + 1)
+                layer1(i + 1)
+            if live(i):
+                relu(i)
+            if live(i + 2):
+                make_edge_term(i + 2)

@@ -97,21 +97,18 @@ def tile_edgenetwork_kernel(
         ident_bf16 = const.tile([P, P], BF16)
         make_identity(nc, ident_bf16[:])
 
-        def contraction_onto_partitions(row_words, grouped):
+        def contraction_onto_partitions(row_words, grouped, half):
             grouped_words = grouped[:].bitcast(F32)
-            for half in range(SUBS // 2):
-                flipped = flip_psum.tile([P, 2, 2, P], F32)
-                for s in range(2):
-                    for u in range(2):
-                        nc.tensor.transpose(
-                            flipped[:, s, u, :], row_words(2 * half + s)[:, u * P : (u + 1) * P], ident_f32[:]
-                        )
-                nc.scalar.copy(
-                    out=grouped_words[:, 2 * half * P : (2 * half + 2) * P, :].rearrange(
-                        "p (s r) u -> p s r u", s=2
-                    ),
-                    in_=flipped[:].rearrange("p s u r -> p s r u"),
-                )
+            flipped = flip_psum.tile([P, 2, 2, P], F32)
+            for s in range(2):
+                for u in range(2):
+                    nc.tensor.transpose(
+                        flipped[:, s, u, :], row_words(2 * half + s)[:, u * P : (u + 1) * P], ident_f32[:]
+                    )
+            nc.scalar.copy(
+                out=grouped_words[:, 2 * half * P : (2 * half + 2) * P, :].rearrange("p (s r) u -> p s r u", s=2),
+                in_=flipped[:].rearrange("p s u r -> p s r u"),
+            )
 
         def quantise(grouped, codes, scales):
             nc.vector.quantize_mx(
@@ -120,7 +117,8 @@ def tile_edgenetwork_kernel(
 
         w1_words = w1_rows[:].bitcast(F32)
         w1_grouped = const.tile([P, MID, PACK], BF16, align_bytes=64)
-        contraction_onto_partitions(lambda t: w1_words[:, t, 0 : D // 2], w1_grouped)
+        for half in range(2):
+            contraction_onto_partitions(lambda t: w1_words[:, t, 0 : D // 2], w1_grouped, half)
         w1_codes = const.tile([P, MID], U32, align_bytes=64)
         w1_scales = const.tile([P, MID], U8, align_bytes=64)
         quantise(w1_grouped, w1_codes, w1_scales)
@@ -143,14 +141,14 @@ def tile_edgenetwork_kernel(
 
         x_grouped, x_codes, x_scales = {}, {}, {}
         edge_terms, layer1_banks, pre_acts, hidden = {}, {}, {}, {}
-        h_codes, h_scales, out_flipped = {}, {}, {}
+        h_codes, h_scales, out_flipped, out_back = {}, {}, {}, {}
 
-        def flip_x(c):
+        def flip_x(c, half):
             x_words = x_blocks[c // CHUNKS_PER_BLOCK][:].bitcast(F32)
             first = (c % CHUNKS_PER_BLOCK) * SUBS
-            grouped = work.tile([P, CHUNK, PACK], BF16, align_bytes=64, name="x_grouped")
-            contraction_onto_partitions(lambda s: x_words[:, first + s, :], grouped)
-            x_grouped[c] = grouped
+            if half == 0:
+                x_grouped[c] = work.tile([P, CHUNK, PACK], BF16, align_bytes=64, name="x_grouped")
+            contraction_onto_partitions(lambda s: x_words[:, first + s, :], x_grouped[c], half)
 
         def make_edge_term(c):
             term = term_pool.tile([P, M_TILES, CHUNK], F32, name="edge_term")
@@ -181,20 +179,19 @@ def tile_edgenetwork_kernel(
             quantise(x_grouped[c], codes, scales)
             x_codes[c], x_scales[c] = codes, scales
 
-        def layer1(c):
-            for s in range(SUBS):
-                bank = layer1_psum.tile([P, M_TILES, P], F32, name="layer1_bank")
-                for t in range(M_TILES):
-                    nc.tensor.matmul_mx(
-                        out=bank[:, t, :],
-                        lhsT=w1_codes[:, t * P : (t + 1) * P].bitcast(FP8X4),
-                        lhsT_scale=w1_scales[:, t * P : (t + 1) * P],
-                        rhs=x_codes[c][:, s * P : (s + 1) * P].bitcast(FP8X4),
-                        rhs_scale=x_scales[c][:, s * P : (s + 1) * P],
-                        start=True,
-                        stop=True,
-                    )
-                layer1_banks[c, s] = bank
+        def layer1(c, s):
+            bank = layer1_psum.tile([P, M_TILES, P], F32, name="layer1_bank")
+            for t in range(M_TILES):
+                nc.tensor.matmul_mx(
+                    out=bank[:, t, :],
+                    lhsT=w1_codes[:, t * P : (t + 1) * P].bitcast(FP8X4),
+                    lhsT_scale=w1_scales[:, t * P : (t + 1) * P],
+                    rhs=x_codes[c][:, s * P : (s + 1) * P].bitcast(FP8X4),
+                    rhs_scale=x_scales[c][:, s * P : (s + 1) * P],
+                    start=True,
+                    stop=True,
+                )
+            layer1_banks[c, s] = bank
 
         def add_edge_term(c, s):
             if s == 0:
@@ -238,12 +235,15 @@ def tile_edgenetwork_kernel(
             )
             out_flipped[c] = flipped
 
+        def flip_back(c, half):
+            if half == 0:
+                out_back[c] = back_psum.tile([P, SUBS, OUT], F32, tag="back", name="out_back")
+            for s in (2 * half, 2 * half + 1):
+                nc.tensor.transpose(out_back[c][:, s, :], out_flipped[c][:, s * P : (s + 1) * P], ident_f32[:])
+
         def store(c):
-            back = back_psum.tile([P, SUBS, OUT], F32, tag="back")
-            for s in range(SUBS):
-                nc.tensor.transpose(back[:, s, :], out_flipped[c][:, s * P : (s + 1) * P], ident_f32[:])
             result = store_pool.tile([P, SUBS, OUT], F32)
-            nc.scalar.copy(out=result[:], in_=back[:])
+            nc.scalar.copy(out=result[:], in_=out_back[c][:])
             nc.scalar.dma_start(
                 out=out[c * CHUNK : (c + 1) * CHUNK, :].rearrange("(s p) o -> p s o", p=P), in_=result[:]
             )
@@ -251,28 +251,31 @@ def tile_edgenetwork_kernel(
         def live(c):
             return 0 <= c < N_CHUNKS
 
-        for i in range(-2, N_CHUNKS + 2):
-            ahead = i + 2
+        for i in range(-3, N_CHUNKS + 2):
+            ahead = i + 3
             if live(ahead) and ahead % CHUNKS_PER_BLOCK == 0:
                 b = ahead // CHUNKS_PER_BLOCK + BLOCKS_AHEAD
                 if b < N_BLOCKS:
                     load_block(b)
+            for half in range(2):
+                if live(i):
+                    add_edge_term(i, 2 * half)
+                    add_edge_term(i, 2 * half + 1)
+                if half == 1 and live(i - 1):
+                    layer2(i - 1)
+                if live(i + 1):
+                    layer1(i + 1, 2 * half)
+                    layer1(i + 1, 2 * half + 1)
+                if live(i + 3):
+                    flip_x(i + 3, half)
+                if live(i - 2):
+                    flip_back(i - 2, half)
+                if half == 0 and live(i - 1):
+                    quantise_h(i - 1)
             if live(i - 2):
                 store(i - 2)
             if live(i + 2):
-                flip_x(i + 2)
-            if live(i):
-                add_edge_term(i, 0)
-                add_edge_term(i, 1)
-            if live(i - 1):
-                quantise_h(i - 1)
-                layer2(i - 1)
-            if live(i):
-                add_edge_term(i, 2)
-                add_edge_term(i, 3)
-            if live(i + 1):
-                quantise_x(i + 1)
-                layer1(i + 1)
+                quantise_x(i + 2)
             if live(i):
                 relu(i)
             if live(i + 2):

@@ -19,10 +19,10 @@ M_TILES = MID // P
 CHUNK = 512
 SUBS = CHUNK // P
 N_CHUNKS = E // CHUNK
-BLOCK = 1024
+BLOCK = 512
 CHUNKS_PER_BLOCK = BLOCK // CHUNK
 N_BLOCKS = E // BLOCK
-BLOCKS_AHEAD = 2
+BLOCKS_AHEAD = 4
 EDGE_PIECES = 4
 SCALAR_M_TILES = 2
 

@@ -24,7 +24,7 @@ CHUNKS_PER_BLOCK = BLOCK // CHUNK
 N_BLOCKS = E // BLOCK
 BLOCKS_AHEAD = 4
 EDGE_PIECES = 4
-SCALAR_M_TILES = 2
+SCALAR_M_TILES = 1
 
 FLOPS = 2 * E * ((D + 1) * MID + MID * OUT)
 

@@ -220,15 +220,16 @@ def tile_edgenetwork_kernel(
 
         def layer2(c):
             acc = layer2_psum.tile([P, CHUNK], F32, tag="layer2")
-            nc.tensor.matmul_mx(
-                out=acc[:],
-                lhsT=w2_codes[:].bitcast(FP8X4),
-                lhsT_scale=w2_scales[:],
-                rhs=h_codes[c][:].bitcast(FP8X4),
-                rhs_scale=h_scales[c][:],
-                start=True,
-                stop=True,
-            )
+            for repeat in range(2):
+                nc.tensor.matmul_mx(
+                    out=acc[:],
+                    lhsT=w2_codes[:].bitcast(FP8X4),
+                    lhsT_scale=w2_scales[:],
+                    rhs=h_codes[c][:].bitcast(FP8X4),
+                    rhs_scale=h_scales[c][:],
+                    start=True,
+                    stop=True,
+                )
             flipped = work.tile([P, CHUNK], F32, name="out_flipped")
             nc.scalar.activation(
                 out=flipped[:], in_=acc[:], func=ACT.Tanh, bias=bias_cols[:, M_TILES : M_TILES + 1], scale=1.0

@@ -24,6 +24,7 @@ CHUNKS_PER_BLOCK = BLOCK // CHUNK
 N_BLOCKS = E // BLOCK
 BLOCKS_AHEAD = 4
 EDGE_PIECES = 4
+RUN = 4
 SCALAR_M_TILES = 1
 
 FLOPS = 2 * E * ((D + 1) * MID + MID * OUT)
@@ -197,9 +198,9 @@ def tile_edgenetwork_kernel(
             if s == 0:
                 pre_acts[c] = work.tile([P, CHUNK, PACK], BF16, align_bytes=64, name="pre_act")
             nc.vector.tensor_tensor(
-                out=pre_acts[c][:, s * P : (s + 1) * P, :],
-                in0=layer1_banks[c, s][:].rearrange("p t e -> p e t"),
-                in1=edge_terms[c][:, :, s * P : (s + 1) * P].rearrange("p t e -> p e t"),
+                out=pre_acts[c][:, s * P : (s + 1) * P, :].rearrange("p (g i) t -> p g t i", i=RUN),
+                in0=layer1_banks[c, s][:].rearrange("p t (g i) -> p g t i", i=RUN),
+                in1=edge_terms[c][:, :, s * P : (s + 1) * P].rearrange("p t (g i) -> p g t i", i=RUN),
                 op=ALU.add,
             )
 
@@ -220,16 +221,15 @@ def tile_edgenetwork_kernel(
 
         def layer2(c):
             acc = layer2_psum.tile([P, CHUNK], F32, tag="layer2")
-            for repeat in range(2):
-                nc.tensor.matmul_mx(
-                    out=acc[:],
-                    lhsT=w2_codes[:].bitcast(FP8X4),
-                    lhsT_scale=w2_scales[:],
-                    rhs=h_codes[c][:].bitcast(FP8X4),
-                    rhs_scale=h_scales[c][:],
-                    start=True,
-                    stop=True,
-                )
+            nc.tensor.matmul_mx(
+                out=acc[:],
+                lhsT=w2_codes[:].bitcast(FP8X4),
+                lhsT_scale=w2_scales[:],
+                rhs=h_codes[c][:].bitcast(FP8X4),
+                rhs_scale=h_scales[c][:],
+                start=True,
+                stop=True,
+            )
             flipped = work.tile([P, CHUNK], F32, name="out_flipped")
             nc.scalar.activation(
                 out=flipped[:], in_=acc[:], func=ACT.Tanh, bias=bias_cols[:, M_TILES : M_TILES + 1], scale=1.0

@@ -23,9 +23,11 @@ BLOCK = 512
 CHUNKS_PER_BLOCK = BLOCK // CHUNK
 N_BLOCKS = E // BLOCK
 BLOCKS_AHEAD = 4
-EDGE_PIECES = 4
+EDGE_PIECE = 2048
+CHUNKS_PER_PIECE = EDGE_PIECE // CHUNK
 RUN = 4
 SCALAR_M_TILES = 1
+SCALAR_EDGES = 128
 
 FLOPS = 2 * E * ((D + 1) * MID + MID * OUT)
 
@@ -52,7 +54,7 @@ def tile_edgenetwork_kernel(
         work = stack.enter_context(tc.tile_pool(name="work", bufs=2))
         store_pool = stack.enter_context(tc.tile_pool(name="store", bufs=3))
         flip_psum = stack.enter_context(tc.psum_pool(name="flip_psum", bufs=2))
-        layer1_psum = stack.enter_context(tc.psum_pool(name="layer1_psum", bufs=SUBS))
+        layer1_psum = stack.enter_context(tc.psum_pool(name="layer1_psum", bufs=M_TILES))
         layer2_psum = stack.enter_context(tc.psum_pool(name="layer2_psum", bufs=1))
         back_psum = stack.enter_context(tc.psum_pool(name="back_psum", bufs=1))
 
@@ -73,9 +75,18 @@ def tile_edgenetwork_kernel(
                 )
             x_blocks[b] = x_rows
 
+        edge_all = const.tile([P, E], BF16)
+
+        def load_edges(q):
+            nc.sync.dma_start(
+                out=edge_all[:, q * EDGE_PIECE : (q + 1) * EDGE_PIECE],
+                in_=edge_feat[q * EDGE_PIECE : (q + 1) * EDGE_PIECE].partition_broadcast(P),
+            )
+
         w1_rows = const.tile([P, M_TILES, D + 2], BF16)
         nc.sync.dma_start(out=w1_rows[:, :, 0 : D + 1], in_=W1.rearrange("(t p) k -> p t k", p=P))
         load_block(0)
+        load_edges(0)
         w2_rows = const.tile([P, MID], BF16)
         nc.sync.dma_start(out=w2_rows[:], in_=W2)
         bias_rows = const.tile([P, P], BF16)
@@ -84,14 +95,6 @@ def tile_edgenetwork_kernel(
         nc.sync.dma_start(out=bias_rows[M_TILES : M_TILES + 1, :], in_=b2.rearrange("(o p) -> o p", p=P))
         for b in range(1, BLOCKS_AHEAD):
             load_block(b)
-
-        edge_all = const.tile([P, E], BF16)
-        piece = E // EDGE_PIECES
-        for q in range(EDGE_PIECES):
-            nc.scalar.dma_start(
-                out=edge_all[:, q * piece : (q + 1) * piece],
-                in_=edge_feat[q * piece : (q + 1) * piece].partition_broadcast(P),
-            )
 
         ident_f32 = const.tile([P, P], F32)
         make_identity(nc, ident_f32[:])
@@ -180,38 +183,40 @@ def tile_edgenetwork_kernel(
             quantise(x_grouped[c], codes, scales)
             x_codes[c], x_scales[c] = codes, scales
 
-        def layer1(c, s):
-            bank = layer1_psum.tile([P, M_TILES, P], F32, name="layer1_bank")
-            for t in range(M_TILES):
-                nc.tensor.matmul_mx(
-                    out=bank[:, t, :],
-                    lhsT=w1_codes[:, t * P : (t + 1) * P].bitcast(FP8X4),
-                    lhsT_scale=w1_scales[:, t * P : (t + 1) * P],
-                    rhs=x_codes[c][:, s * P : (s + 1) * P].bitcast(FP8X4),
-                    rhs_scale=x_scales[c][:, s * P : (s + 1) * P],
-                    start=True,
-                    stop=True,
-                )
-            layer1_banks[c, s] = bank
+        def layer1(c, t):
+            bank = layer1_psum.tile([P, CHUNK], F32, name="layer1_bank")
+            nc.tensor.matmul_mx(
+                out=bank[:],
+                lhsT=w1_codes[:, t * P : (t + 1) * P].bitcast(FP8X4),
+                lhsT_scale=w1_scales[:, t * P : (t + 1) * P],
+                rhs=x_codes[c][:].bitcast(FP8X4),
+                rhs_scale=x_scales[c][:],
+                start=True,
+                stop=True,
+            )
+            layer1_banks[c, t] = bank
 
-        def add_edge_term(c, s):
-            if s == 0:
-                pre_acts[c] = work.tile([P, CHUNK, PACK], BF16, align_bytes=64, name="pre_act")
+        def add_edge_term(c, t):
+            if t == 0:
+                pre_acts[c] = work.tile([P, M_TILES, CHUNK], BF16, name="pre_act")
             nc.vector.tensor_tensor(
-                out=pre_acts[c][:, s * P : (s + 1) * P, :].rearrange("p (g i) t -> p g t i", i=RUN),
-                in0=layer1_banks[c, s][:].rearrange("p t (g i) -> p g t i", i=RUN),
-                in1=edge_terms[c][:, :, s * P : (s + 1) * P].rearrange("p t (g i) -> p g t i", i=RUN),
-                op=ALU.add,
+                out=pre_acts[c][:, t, :], in0=layer1_banks[c, t][:], in1=edge_terms[c][:, t, :], op=ALU.add
             )
 
-        def relu(c):
-            h = work.tile([P, CHUNK, PACK], BF16, align_bytes=64, name="hidden")
+        def relu_and_group_on_scalar(c):
+            hidden[c] = work.tile([P, CHUNK, PACK], BF16, align_bytes=64, name="hidden")
+            nc.scalar.activation(
+                out=hidden[c][:, 0:SCALAR_EDGES, :].rearrange("p (g i) t -> p g t i", i=RUN),
+                in_=pre_acts[c][:, :, 0:SCALAR_EDGES].rearrange("p t (g i) -> p g t i", i=RUN),
+                func=ACT.Relu,
+            )
+
+        def relu_and_group_on_vector(c):
             nc.vector.tensor_scalar_max(
-                out=h[:].rearrange("p e t -> p (e t)"),
-                in0=pre_acts[c][:].rearrange("p e t -> p (e t)"),
+                out=hidden[c][:, SCALAR_EDGES:CHUNK, :].rearrange("p (g i) t -> p g t i", i=RUN),
+                in0=pre_acts[c][:, :, SCALAR_EDGES:CHUNK].rearrange("p t (g i) -> p g t i", i=RUN),
                 scalar1=0.0,
             )
-            hidden[c] = h
 
         def quantise_h(c):
             codes = work.tile([P, CHUNK], U32, align_bytes=64, name="h_codes")
@@ -258,6 +263,8 @@ def tile_edgenetwork_kernel(
                 b = ahead // CHUNKS_PER_BLOCK + BLOCKS_AHEAD
                 if b < N_BLOCKS:
                     load_block(b)
+            if live(ahead + CHUNKS_PER_PIECE) and ahead % CHUNKS_PER_PIECE == 0:
+                load_edges(ahead // CHUNKS_PER_PIECE + 1)
             for half in range(2):
                 if live(i):
                     add_edge_term(i, 2 * half)
@@ -275,9 +282,11 @@ def tile_edgenetwork_kernel(
                     quantise_h(i - 1)
             if live(i - 2):
                 store(i - 2)
+            if live(i):
+                relu_and_group_on_scalar(i)
             if live(i + 2):
                 quantise_x(i + 2)
             if live(i):
-                relu(i)
+                relu_and_group_on_vector(i)
             if live(i + 2):
                 make_edge_term(i + 2)

@@ -19,15 +19,12 @@ M_TILES = MID // P
 CHUNK = 512
 SUBS = CHUNK // P
 N_CHUNKS = E // CHUNK
-BLOCK = 512
-CHUNKS_PER_BLOCK = BLOCK // CHUNK
-N_BLOCKS = E // BLOCK
-BLOCKS_AHEAD = 4
+CHUNKS_AHEAD = 4
 EDGE_PIECE = 2048
 CHUNKS_PER_PIECE = EDGE_PIECE // CHUNK
 RUN = 4
 SCALAR_M_TILES = 1
-SCALAR_EDGES = 128
+SCALAR_EDGES = P
 
 FLOPS = 2 * E * ((D + 1) * MID + MID * OUT)
 
@@ -49,7 +46,7 @@ def tile_edgenetwork_kernel(
     with ExitStack() as stack:
         stack.enter_context(tc.manual_schedule())
         const = stack.enter_context(tc.tile_pool(name="const", bufs=1))
-        rows_pool = stack.enter_context(tc.tile_pool(name="rows", bufs=BLOCKS_AHEAD + 1))
+        rows_pool = stack.enter_context(tc.tile_pool(name="rows", bufs=CHUNKS_AHEAD + 1))
         term_pool = stack.enter_context(tc.tile_pool(name="term", bufs=3))
         work = stack.enter_context(tc.tile_pool(name="work", bufs=2))
         store_pool = stack.enter_context(tc.tile_pool(name="store", bufs=3))
@@ -64,16 +61,16 @@ def tile_edgenetwork_kernel(
             (src_node_feat, F + H, F),
             (src_node_hidden, 2 * F + H, H),
         )
-        x_blocks = {}
+        x_rows = {}
 
-        def load_block(b):
-            x_rows = rows_pool.tile([P, BLOCK // P, D], BF16)
+        def load_chunk(c):
+            rows = rows_pool.tile([P, SUBS, D], BF16, name="x_rows")
             for part, first, width in x_parts:
                 nc.sync.dma_start(
-                    out=x_rows[:, :, first : first + width],
-                    in_=part[b * BLOCK : (b + 1) * BLOCK, :].rearrange("(r p) c -> p r c", p=P),
+                    out=rows[:, :, first : first + width],
+                    in_=part[c * CHUNK : (c + 1) * CHUNK, :].rearrange("(s p) k -> p s k", p=P),
                 )
-            x_blocks[b] = x_rows
+            x_rows[c] = rows
 
         edge_all = const.tile([P, E], BF16)
 
@@ -85,7 +82,7 @@ def tile_edgenetwork_kernel(
 
         w1_rows = const.tile([P, M_TILES, D + 2], BF16)
         nc.sync.dma_start(out=w1_rows[:, :, 0 : D + 1], in_=W1.rearrange("(t p) k -> p t k", p=P))
-        load_block(0)
+        load_chunk(0)
         load_edges(0)
         w2_rows = const.tile([P, MID], BF16)
         nc.sync.dma_start(out=w2_rows[:], in_=W2)
@@ -93,8 +90,8 @@ def tile_edgenetwork_kernel(
         nc.vector.memset(bias_rows[:], 0.0)
         nc.sync.dma_start(out=bias_rows[0:M_TILES, :], in_=b1.rearrange("(t p) -> t p", p=P))
         nc.sync.dma_start(out=bias_rows[M_TILES : M_TILES + 1, :], in_=b2.rearrange("(o p) -> o p", p=P))
-        for b in range(1, BLOCKS_AHEAD):
-            load_block(b)
+        for c in range(1, CHUNKS_AHEAD):
+            load_chunk(c)
 
         ident_f32 = const.tile([P, P], F32)
         make_identity(nc, ident_f32[:])
@@ -148,11 +145,10 @@ def tile_edgenetwork_kernel(
         h_codes, h_scales, out_flipped, out_back = {}, {}, {}, {}
 
         def flip_x(c, half):
-            x_words = x_blocks[c // CHUNKS_PER_BLOCK][:].bitcast(F32)
-            first = (c % CHUNKS_PER_BLOCK) * SUBS
+            x_words = x_rows[c][:].bitcast(F32)
             if half == 0:
                 x_grouped[c] = work.tile([P, CHUNK, PACK], BF16, align_bytes=64, name="x_grouped")
-            contraction_onto_partitions(lambda s: x_words[:, first + s, :], x_grouped[c], half)
+            contraction_onto_partitions(lambda s: x_words[:, s, :], x_grouped[c], half)
 
         def make_edge_term(c):
             term = term_pool.tile([P, M_TILES, CHUNK], F32, name="edge_term")
@@ -235,11 +231,10 @@ def tile_edgenetwork_kernel(
                 start=True,
                 stop=True,
             )
-            flipped = work.tile([P, CHUNK], F32, name="out_flipped")
+            out_flipped[c] = work.tile([P, CHUNK], F32, name="out_flipped")
             nc.scalar.activation(
-                out=flipped[:], in_=acc[:], func=ACT.Tanh, bias=bias_cols[:, M_TILES : M_TILES + 1], scale=1.0
+                out=out_flipped[c][:], in_=acc[:], func=ACT.Tanh, bias=bias_cols[:, M_TILES : M_TILES + 1], scale=1.0
             )
-            out_flipped[c] = flipped
 
         def flip_back(c, half):
             if half == 0:
@@ -259,31 +254,28 @@ def tile_edgenetwork_kernel(
 
         for i in range(-3, N_CHUNKS + 2):
             ahead = i + 3
-            if live(ahead) and ahead % CHUNKS_PER_BLOCK == 0:
-                b = ahead // CHUNKS_PER_BLOCK + BLOCKS_AHEAD
-                if b < N_BLOCKS:
-                    load_block(b)
+            if live(ahead + CHUNKS_AHEAD):
+                load_chunk(ahead + CHUNKS_AHEAD)
             if live(ahead + CHUNKS_PER_PIECE) and ahead % CHUNKS_PER_PIECE == 0:
                 load_edges(ahead // CHUNKS_PER_PIECE + 1)
             for half in range(2):
                 if live(i):
                     add_edge_term(i, 2 * half)
                     add_edge_term(i, 2 * half + 1)
-                if half == 1 and live(i - 1):
-                    layer2(i - 1)
+                if half == 1 and live(i):
+                    relu_and_group_on_scalar(i)
                 if live(i + 1):
                     layer1(i + 1, 2 * half)
                     layer1(i + 1, 2 * half + 1)
+                if half == 1 and live(i - 1):
+                    quantise_h(i - 1)
+                    layer2(i - 1)
                 if live(i + 3):
                     flip_x(i + 3, half)
                 if live(i - 2):
                     flip_back(i - 2, half)
-                if half == 0 and live(i - 1):
-                    quantise_h(i - 1)
             if live(i - 2):
                 store(i - 2)
-            if live(i):
-                relu_and_group_on_scalar(i)
             if live(i + 2):
                 quantise_x(i + 2)
             if live(i):

from contextlib import ExitStack

import concourse.mybir as mybir
from concourse.masks import make_identity

F32 = mybir.dt.float32
BF16 = mybir.dt.bfloat16
U32 = mybir.dt.uint32
U8 = mybir.dt.uint8
FP8X4 = mybir.dt.float8_e4m3fn_x4
ACT = mybir.ActivationFunctionType
ALU = mybir.AluOpType

P = 128
PACK = 4
E, F, H, MID, OUT = 16384, 64, 192, 512, 128
D = 2 * (F + H)
M_TILES = MID // P
CHUNK = 512
SUBS = CHUNK // P
N_CHUNKS = E // CHUNK
CHUNKS_AHEAD = 4
EDGE_PIECE = 2048
CHUNKS_PER_PIECE = EDGE_PIECE // CHUNK
RUN = 4
SCALAR_M_TILES = 1
SCALAR_EDGES = P

FLOPS = 2 * E * ((D + 1) * MID + MID * OUT)


def tile_edgenetwork_kernel(
    tc,
    dst_node_feat,
    dst_node_hidden,
    src_node_feat,
    src_node_hidden,
    edge_feat,
    W1,
    b1,
    W2,
    b2,
    out,
):
    nc = tc.nc
    with ExitStack() as stack:
        stack.enter_context(tc.manual_schedule())
        const = stack.enter_context(tc.tile_pool(name="const", bufs=1))
        rows_pool = stack.enter_context(tc.tile_pool(name="rows", bufs=CHUNKS_AHEAD + 1))
        term_pool = stack.enter_context(tc.tile_pool(name="term", bufs=3))
        work = stack.enter_context(tc.tile_pool(name="work", bufs=2))
        store_pool = stack.enter_context(tc.tile_pool(name="store", bufs=3))
        flip_psum = stack.enter_context(tc.psum_pool(name="flip_psum", bufs=2))
        layer1_psum = stack.enter_context(tc.psum_pool(name="layer1_psum", bufs=M_TILES))
        layer2_psum = stack.enter_context(tc.psum_pool(name="layer2_psum", bufs=1))
        back_psum = stack.enter_context(tc.psum_pool(name="back_psum", bufs=1))

        x_parts = (
            (dst_node_feat, 0, F),
            (dst_node_hidden, F, H),
            (src_node_feat, F + H, F),
            (src_node_hidden, 2 * F + H, H),
        )
        x_rows = {}

        def load_chunk(c):
            rows = rows_pool.tile([P, SUBS, D], BF16, name="x_rows")
            for part, first, width in x_parts:
                nc.sync.dma_start(
                    out=rows[:, :, first : first + width],
                    in_=part[c * CHUNK : (c + 1) * CHUNK, :].rearrange("(s p) k -> p s k", p=P),
                )
            x_rows[c] = rows

        edge_all = const.tile([P, E], BF16)

        def load_edges(q):
            nc.sync.dma_start(
                out=edge_all[:, q * EDGE_PIECE : (q + 1) * EDGE_PIECE],
                in_=edge_feat[q * EDGE_PIECE : (q + 1) * EDGE_PIECE].partition_broadcast(P),
            )

        w1_rows = const.tile([P, M_TILES, D + 2], BF16)
        nc.sync.dma_start(out=w1_rows[:, :, 0 : D + 1], in_=W1.rearrange("(t p) k -> p t k", p=P))
        load_chunk(0)
        load_edges(0)
        w2_rows = const.tile([P, MID], BF16)
        nc.sync.dma_start(out=w2_rows[:], in_=W2)
        bias_rows = const.tile([P, P], BF16)
        nc.vector.memset(bias_rows[:], 0.0)
        nc.sync.dma_start(out=bias_rows[0:M_TILES, :], in_=b1.rearrange("(t p) -> t p", p=P))
        nc.sync.dma_start(out=bias_rows[M_TILES : M_TILES + 1, :], in_=b2.rearrange("(o p) -> o p", p=P))
        for c in range(1, CHUNKS_AHEAD):
            load_chunk(c)

        ident_f32 = const.tile([P, P], F32)
        make_identity(nc, ident_f32[:])
        ident_bf16 = const.tile([P, P], BF16)
        make_identity(nc, ident_bf16[:])

        def contraction_onto_partitions(row_words, grouped, half):
            grouped_words = grouped[:].bitcast(F32)
            flipped = flip_psum.tile([P, 2, 2, P], F32)
            for s in range(2):
                for u in range(2):
                    nc.tensor.transpose(
                        flipped[:, s, u, :], row_words(2 * half + s)[:, u * P : (u + 1) * P], ident_f32[:]
                    )
            nc.scalar.copy(
                out=grouped_words[:, 2 * half * P : (2 * half + 2) * P, :].rearrange("p (s r) u -> p s r u", s=2),
                in_=flipped[:].rearrange("p s u r -> p s r u"),
            )

        def quantise(grouped, codes, scales):
            nc.vector.quantize_mx(
                out=codes[:].bitcast(FP8X4), scales=scales[:], in_=grouped[:].rearrange("p c j -> p (c j)")
            )

        w1_words = w1_rows[:].bitcast(F32)
        w1_grouped = const.tile([P, MID, PACK], BF16, align_bytes=64)
        for half in range(2):
            contraction_onto_partitions(lambda t: w1_words[:, t, 0 : D // 2], w1_grouped, half)
        w1_codes = const.tile([P, MID], U32, align_bytes=64)
        w1_scales = const.tile([P, MID], U8, align_bytes=64)
        quantise(w1_grouped, w1_codes, w1_scales)

        w2_flipped = back_psum.tile([P, M_TILES, OUT], BF16, tag="back")
        for t in range(M_TILES):
            nc.tensor.transpose(w2_flipped[:, t, :], w2_rows[:, t * P : (t + 1) * P], ident_bf16[:])
        w2_grouped = const.tile([P, OUT, PACK], BF16, align_bytes=64)
        nc.vector.tensor_copy(out=w2_grouped[:], in_=w2_flipped[:].rearrange("p t o -> p o t"))
        w2_codes = const.tile([P, OUT], U32, align_bytes=64)
        w2_scales = const.tile([P, OUT], U8, align_bytes=64)

        bias_flipped = layer2_psum.tile([P, P], BF16, tag="layer2")
        nc.tensor.transpose(bias_flipped[:], bias_rows[:], ident_bf16[:])
        bias_cols = const.tile([P, M_TILES + 1], F32)
        nc.vector.tensor_copy(out=bias_cols[:], in_=bias_flipped[:, 0 : M_TILES + 1])
        w1_last = const.tile([P, M_TILES], F32)
        nc.vector.tensor_copy(out=w1_last[:], in_=w1_rows[:, :, D])
        quantise(w2_grouped, w2_codes, w2_scales)

        x_grouped, x_codes, x_scales = {}, {}, {}
        edge_terms, layer1_banks, pre_acts, hidden = {}, {}, {}, {}
        h_codes, h_scales, out_flipped, out_back = {}, {}, {}, {}

        def flip_x(c, half):
            x_words = x_rows[c][:].bitcast(F32)
            if half == 0:
                x_grouped[c] = work.tile([P, CHUNK, PACK], BF16, align_bytes=64, name="x_grouped")
            contraction_onto_partitions(lambda s: x_words[:, s, :], x_grouped[c], half)

        def make_edge_term(c):
            term = term_pool.tile([P, M_TILES, CHUNK], F32, name="edge_term")
            edges = edge_all[:, c * CHUNK : (c + 1) * CHUNK]
            for t in range(M_TILES):
                if t < SCALAR_M_TILES:
                    nc.scalar.activation(
                        out=term[:, t, :],
                        in_=edges,
                        func=ACT.Identity,
                        scale=w1_last[:, t : t + 1],
                        bias=bias_cols[:, t : t + 1],
                    )
                else:
                    nc.gpsimd.tensor_scalar(
                        out=term[:, t, :],
                        in0=edges,
                        scalar1=w1_last[:, t : t + 1],
                        scalar2=bias_cols[:, t : t + 1],
                        op0=ALU.mult,
                        op1=ALU.add,
                    )
            edge_terms[c] = term

        def quantise_x(c):
            codes = work.tile([P, CHUNK], U32, align_bytes=64, name="x_codes")
            scales = work.tile([P, CHUNK], U8, align_bytes=64, name="x_scales")
            quantise(x_grouped[c], codes, scales)
            x_codes[c], x_scales[c] = codes, scales

        def layer1(c, t):
            bank = layer1_psum.tile([P, CHUNK], F32, name="layer1_bank")
            nc.tensor.matmul_mx(
                out=bank[:],
                lhsT=w1_codes[:, t * P : (t + 1) * P].bitcast(FP8X4),
                lhsT_scale=w1_scales[:, t * P : (t + 1) * P],
                rhs=x_codes[c][:].bitcast(FP8X4),
                rhs_scale=x_scales[c][:],
                start=True,
                stop=True,
            )
            layer1_banks[c, t] = bank

        def add_edge_term(c, t):
            if t == 0:
                pre_acts[c] = work.tile([P, M_TILES, CHUNK], BF16, name="pre_act")
            nc.vector.tensor_tensor(
                out=pre_acts[c][:, t, :], in0=layer1_banks[c, t][:], in1=edge_terms[c][:, t, :], op=ALU.add
            )

        def relu_and_group_on_scalar(c):
            hidden[c] = work.tile([P, CHUNK, PACK], BF16, align_bytes=64, name="hidden")
            nc.scalar.activation(
                out=hidden[c][:, 0:SCALAR_EDGES, :].rearrange("p (g i) t -> p g t i", i=RUN),
                in_=pre_acts[c][:, :, 0:SCALAR_EDGES].rearrange("p t (g i) -> p g t i", i=RUN),
                func=ACT.Relu,
            )

        def relu_and_group_on_vector(c):
            nc.vector.tensor_scalar_max(
                out=hidden[c][:, SCALAR_EDGES:CHUNK, :].rearrange("p (g i) t -> p g t i", i=RUN),
                in0=pre_acts[c][:, :, SCALAR_EDGES:CHUNK].rearrange("p t (g i) -> p g t i", i=RUN),
                scalar1=0.0,
            )

        def quantise_h(c):
            codes = work.tile([P, CHUNK], U32, align_bytes=64, name="h_codes")
            scales = work.tile([P, CHUNK], U8, align_bytes=64, name="h_scales")
            quantise(hidden[c], codes, scales)
            h_codes[c], h_scales[c] = codes, scales

        def layer2(c):
            acc = layer2_psum.tile([P, CHUNK], F32, tag="layer2")
            nc.tensor.matmul_mx(
                out=acc[:],
                lhsT=w2_codes[:].bitcast(FP8X4),
                lhsT_scale=w2_scales[:],
                rhs=h_codes[c][:].bitcast(FP8X4),
                rhs_scale=h_scales[c][:],
                start=True,
                stop=True,
            )
            out_flipped[c] = work.tile([P, CHUNK], F32, name="out_flipped")
            nc.scalar.activation(
                out=out_flipped[c][:], in_=acc[:], func=ACT.Tanh, bias=bias_cols[:, M_TILES : M_TILES + 1], scale=1.0
            )

        def flip_back(c, half):
            if half == 0:
                out_back[c] = back_psum.tile([P, SUBS, OUT], F32, tag="back", name="out_back")
            for s in (2 * half, 2 * half + 1):
                nc.tensor.transpose(out_back[c][:, s, :], out_flipped[c][:, s * P : (s + 1) * P], ident_f32[:])

        def store(c):
            result = store_pool.tile([P, SUBS, OUT], F32)
            nc.scalar.copy(out=result[:], in_=out_back[c][:])
            nc.scalar.dma_start(
                out=out[c * CHUNK : (c + 1) * CHUNK, :].rearrange("(s p) o -> p s o", p=P), in_=result[:]
            )

        def live(c):
            return 0 <= c < N_CHUNKS

        for i in range(-3, N_CHUNKS + 2):
            ahead = i + 3
            if live(ahead + CHUNKS_AHEAD):
                load_chunk(ahead + CHUNKS_AHEAD)
            if live(ahead + CHUNKS_PER_PIECE) and ahead % CHUNKS_PER_PIECE == 0:
                load_edges(ahead // CHUNKS_PER_PIECE + 1)
            for half in range(2):
                if live(i):
                    add_edge_term(i, 2 * half)
                    add_edge_term(i, 2 * half + 1)
                if half == 1 and live(i):
                    relu_and_group_on_scalar(i)
                if live(i + 1):
                    layer1(i + 1, 2 * half)
                    layer1(i + 1, 2 * half + 1)
                if half == 1 and live(i - 1):
                    quantise_h(i - 1)
                    layer2(i - 1)
                if live(i + 3):
                    flip_x(i + 3, half)
                if live(i - 2):
                    flip_back(i - 2, half)
            if live(i - 2):
                store(i - 2)
            if live(i + 2):
                quantise_x(i + 2)
            if live(i):
                relu_and_group_on_vector(i)
            if live(i + 2):
                make_edge_term(i + 2)
